import numpy as np
import ml_dtypes


def mxq(x, axis, fmt="e4m3"):
    dtype, down = {"e4m3": (ml_dtypes.float8_e4m3fn, 7), "e5m2": (ml_dtypes.float8_e5m2, 14)}[fmt]
    v = np.moveaxis(np.asarray(x, np.float32).astype(ml_dtypes.bfloat16).astype(np.float64), axis, -1)
    blocks = v.reshape(v.shape[:-1] + (-1, 32))
    amax = np.abs(blocks).max(-1, keepdims=True)
    byte = np.maximum(np.where(amax > 0, np.frexp(amax)[1] - 1 + 127, 0) - down, 1)
    scale = np.exp2(byte - 127.0)
    codes = (blocks / scale).astype(np.float32).astype(dtype).astype(np.float64)
    return np.moveaxis((codes * scale).reshape(v.shape), -1, axis)


WIDE = False


def mx_kscale(k):
    if not WIDE:
        return np.ones(k)
    levels = np.array([10, -10, 5, -5, 0])
    a = np.random.permutation(np.resize(levels, k // 512 * 4)).reshape(k // 512, 4)
    idx = np.arange(k)
    return np.exp2(a[idx // 512, idx % 128 // 32])


BF16 = ml_dtypes.bfloat16


def bf(x):
    return np.asarray(x, np.float32).astype(BF16)


def f64(x):
    return np.asarray(x).astype(np.float64)


B, S, D, F, N = 8, 1024, 1024, 512, 128
F2 = 2 * F


def setup_inputs():
    t = mx_kscale(F)
    tt = np.concatenate([t, t])
    return {"freq_rect": bf(np.random.standard_normal((B, S, F2))),
            "processed_mag": bf((1.25 + 0.25 * np.random.standard_normal((B, S, F))) * t),
            "down_w": bf(np.random.standard_normal((N, F2)) / np.sqrt(F2) / tt)}


def reference(freq_rect, processed_mag, down_w):
    fr = f64(freq_rect)
    real, imag = fr[..., :F], fr[..., F:]
    mag = np.sqrt(real * real + imag * imag + 1e-8)
    scale = f64(processed_mag) / (mag + 1e-6)
    freq_rect_new = np.concatenate([real * scale, imag * scale], axis=-1)
    return mxq(freq_rect_new, 2, "e4m3") @ mxq(f64(down_w), 1, "e4m3").T

@@ -1,0 +1,214 @@
+from contextlib import ExitStack
+
+import concourse.mybir as mybir
+from concourse.masks import make_identity
+
+F32 = mybir.dt.float32
+BF16 = mybir.dt.bfloat16
+U32 = mybir.dt.uint32
+U8 = mybir.dt.uint8
+FP8X4 = mybir.dt.float8_e4m3fn_x4
+ACT = mybir.ActivationFunctionType
+ALU = mybir.AluOpType
+
+P = 128
+ROWS = 8192
+K = 1024
+F = 512
+N = 128
+FLOPS = 2 * ROWS * K * N
+NG = ROWS // (4 * P)
+NP = 2 * NG
+EPS_MAG = 1e-8
+EPS_DEN = 1e-6
+KSC = 1.0 / (4.0 * EPS_DEN * EPS_DEN)
+PINNED = True
+IN_BUFS = 6
+
+
+def tile_learnablespectralsinkhorn_pb_t_kernel(tc, freq_rect, processed_mag, down_w, out):
+    nc = tc.nc
+    fr_v = freq_rect.flatten_outer_dims().rearrange("(g p j) k -> g p (j k)", p=P, j=4)
+    m_v = processed_mag.flatten_outer_dims().rearrange("(g p j) f -> g p (j f)", p=P, j=4)
+    out_v = out.flatten_outer_dims().rearrange("(g p j) n -> g p (j n)", p=P, j=4)
+    tl = {}
+    with ExitStack() as ctx:
+        const = ctx.enter_context(tc.tile_pool(name="const", bufs=1))
+        work = ctx.enter_context(tc.tile_pool(name="work", bufs=2))
+        psum = ctx.enter_context(tc.psum_pool(name="psum", bufs=2))
+        if PINNED:
+            ctx.enter_context(tc.manual_schedule())
+
+        eps2 = const.tile([P, 1], F32, name="eps2")
+        nc.vector.memset(eps2[:], EPS_DEN * EPS_DEN)
+        warm = const.tile([P, 1], F32, name="warm")
+        nc.scalar.activation(out=warm[:], in_=eps2[:], func=ACT.Abs_reciprocal_sqrt)
+        ident = const.tile([P, P], F32, name="ident")
+        make_identity(nc, ident[:])
+
+        def load(gi):
+            fr = work.tile([P, 4 * K], BF16, name="fr%d" % gi, tag="fr", bufs=IN_BUFS)
+            nc.sync.dma_start(out=fr[:], in_=fr_v[gi])
+            mg = work.tile([P, 4 * F], BF16, name="mg%d" % gi, tag="mg", bufs=IN_BUFS)
+            nc.sync.dma_start(out=mg[:], in_=m_v[gi])
+            tl[("fr", gi)] = fr
+            tl[("mg", gi)] = mg
+
+        w_sb = const.tile([P, K], BF16, name="w_sb")
+        nc.sync.dma_start(out=w_sb[:], in_=down_w)
+        load(0)
+        load(1)
+        load(2)
+
+        w_ps = psum.tile([P, 4, P], F32, name="w_ps", tag="a1", bufs=2)
+        w_words = w_sb[:].bitcast(F32)
+        for c in range(4):
+            nc.tensor.transpose(out=w_ps[:, c, :], in_=w_words[:, c * P:(c + 1) * P], identity=ident[:])
+        w_grp = const.tile([P, K], BF16, name="w_grp", align_bytes=64)
+        nc.vector.tensor_copy(
+            out=w_grp[:].bitcast(F32).rearrange("p (g n u) -> p g n u", g=2, u=2),
+            in_=w_ps[:].rearrange("p (g u) n -> p g n u", u=2),
+        )
+        w_codes = const.tile([P, 2 * N], U32, name="w_codes", align_bytes=64)
+        w_scales = const.tile([P, 2 * N], U8, name="w_scales", align_bytes=64)
+        nc.vector.quantize_mx(out=w_codes[:].bitcast(FP8X4), scales=w_scales[:], in_=w_grp[:])
+
+        def ok(j):
+            return 0 <= j < NP
+
+        def fr_bank(j, g, tag, bufs):
+            gi, h = divmod(j, 2)
+            words = tl[("fr", gi)][:].bitcast(F32)
+            bank = psum.tile([P, 512], F32, name="%s_%d_%d" % (tag, j, g), tag=tag, bufs=bufs)
+            for u in range(2):
+                for unit in range(2):
+                    col = (2 * h + unit) * 512 + (2 * g + u) * P
+                    dst = (2 * u + unit) * P
+                    nc.tensor.transpose(out=bank[:, dst:dst + P], in_=words[:, col:col + P], identity=ident[:])
+            return bank
+
+        def t1(j):
+            for g in range(2):
+                tl[("a1", j, g)] = fr_bank(j, g, "a1", 2)
+
+        def sq(j):
+            t = work.tile([P, 2048], F32, name="sq%d" % j, tag="sq", bufs=3)
+            for g in range(2):
+                nc.scalar.activation(out=t[:, g * 1024:(g + 1) * 1024], in_=tl[("a1", j, g)][:].bitcast(BF16), func=ACT.Square)
+            tl[("sq", j)] = t
+
+        def ad(j):
+            t = tl[("sq", j)]
+            q = work.tile([P, 1024], F32, name="q%d" % j, tag="q", bufs=4)
+            nc.gpsimd.tensor_tensor(out=q[:], in0=t[:, 0:1024], in1=t[:, 1024:2048], op=ALU.add)
+            nc.gpsimd.tensor_scalar(out=q[:], in0=q[:], scalar1=1.0, scalar2=EPS_MAG, op0=ALU.mult, op1=ALU.add)
+            tl[("q", j)] = q
+
+        def r1(j):
+            z = work.tile([P, 1024], F32, name="z%d" % j, tag="z", bufs=2)
+            nc.scalar.activation(out=z[:], in_=tl[("q", j)][:], func=ACT.Abs_reciprocal_sqrt, scale=KSC)
+            tl[("z", j)] = z
+
+        def st(j):
+            uu = work.tile([P, 1024], F32, name="uu%d" % j, tag="uu", bufs=3)
+            nc.vector.scalar_tensor_tensor(out=uu[:], in0=tl[("z", j)][:], scalar=1.0, in1=tl[("q", j)][:], op0=ALU.add, op1=ALU.mult)
+            tl[("uu", j)] = uu
+
+        def r2(j):
+            d = work.tile([P, 1024], F32, name="d%d" % j, tag="d", bufs=3)
+            nc.scalar.activation(out=d[:], in_=tl[("uu", j)][:], func=ACT.Abs_reciprocal_sqrt, bias=eps2[:])
+            tl[("d", j)] = d
+
+        def t3m(j):
+            gi, h = divmod(j, 2)
+            words = tl[("mg", gi)][:].bitcast(F32)
+            bank = psum.tile([P, 512], F32, name="mt%d" % j, tag="mt", bufs=1)
+            for u in range(2):
+                for unit in range(2):
+                    col = (2 * h + unit) * 256 + u * P
+                    dst = (2 * u + unit) * P
+                    nc.tensor.transpose(out=bank[:, dst:dst + P], in_=words[:, col:col + P], identity=ident[:])
+            tl[("mt", j)] = bank
+
+        def t3a(j):
+            for g in range(2):
+                tl[("a3", j, g)] = fr_bank(j, g, "a3", 3)
+
+        def xm(j):
+            s = work.tile([P, 1024], F32, name="s%d" % j, tag="s", bufs=2)
+            nc.vector.tensor_tensor(out=s[:], in0=tl[("mt", j)][:].bitcast(BF16), in1=tl[("d", j)][:], op=ALU.mult)
+            tl[("s", j)] = s
+
+        def fn(j):
+            grp = work.tile([P, 2048], BF16, name="grp%d" % j, tag="grp", bufs=3, align_bytes=64)
+            s4 = tl[("s", j)][:].rearrange("p (u w e) -> p w u e", u=2, e=2)
+            for g in range(2):
+                nc.vector.tensor_tensor(
+                    out=grp[:, g * 1024:(g + 1) * 1024].rearrange("p (w u e) -> p w u e", u=2, e=2),
+                    in0=tl[("a3", j, g)][:].bitcast(BF16).rearrange("p (u w e) -> p w u e", u=2, e=2),
+                    in1=s4,
+                    op=ALU.mult,
+                )
+            tl[("grp", j)] = grp
+
+        def qz(j):
+            codes = work.tile([P, 512], U32, name="codes%d" % j, tag="codes", bufs=3, align_bytes=64)
+            scales = work.tile([P, 512], U8, name="scales%d" % j, tag="scales", bufs=3, align_bytes=64)
+            nc.vector.quantize_mx(out=codes[:].bitcast(FP8X4), scales=scales[:], in_=tl[("grp", j)][:])
+            tl[("codes", j)] = codes
+            tl[("scales", j)] = scales
+
+        def mx(j):
+            gi, h = divmod(j, 2)
+            if h == 0:
+                tl[("o", gi)] = psum.tile([P, 512], F32, name="o%d" % gi, tag="o", bufs=2)
+            o = tl[("o", gi)]
+            codes = tl[("codes", j)]
+            scales = tl[("scales", j)]
+            for unit in range(2):
+                col = (2 * h + unit) * P
+                for g in range(2):
+                    a = g * 256 + unit * P
+                    nc.tensor.matmul_mx(
+                        out=o[:, col:col + P],
+                        lhsT=codes[:, a:a + P].bitcast(FP8X4),
+                        lhsT_scale=scales[:, a:a + P],
+                        rhs=w_codes[:, g * N:(g + 1) * N].bitcast(FP8X4),
+                        rhs_scale=w_scales[:, g * N:(g + 1) * N],
+                        start=(g == 0),
+                        stop=(g == 1),
+                    )
+
+        def oc(gi):
+            ob = work.tile([P, 512], F32, name="ob%d" % gi, tag="ob", bufs=2)
+            nc.scalar.copy(out=ob[:], in_=tl[("o", gi)][:])
+            nc.sync.dma_start(out=out_v[gi], in_=ob[:])
+
+        t1(0)
+        for t in range(0, NP + 7):
+            if ok(t):
+                sq(t)
+            if ok(t + 1):
+                t1(t + 1)
+            if ok(t):
+                ad(t)
+            if ok(t - 4):
+                xm(t - 4)
+            if ok(t - 3):
+                t3m(t - 3)
+            if ok(t - 5):
+                qz(t - 5)
+                mx(t - 5)
+            if ok(t - 4):
+                fn(t - 4)
+            if ok(t - 3):
+                t3a(t - 3)
+            if ok(t - 2):
+                r1(t - 2)
+                st(t - 2)
+            if ok(t - 3):
+                r2(t - 3)
+            if ok(t - 6) and (t - 6) % 2 == 1:
+                oc((t - 6) // 2)
+            if t % 2 == 0 and t // 2 + 3 < NG:
+                load(t // 2 + 3)

@@ -46,131 +46,156 @@ def tile_learnablespectralsinkhorn_pb_t_kernel(tc, freq_rect, processed_mag, dow
         ident = const.tile([P, P], F32, name="ident")
         make_identity(nc, ident[:])
 
-        def load(gi):
-            fr = work.tile([P, 4 * K], BF16, name="fr%d" % gi, tag="fr", bufs=IN_BUFS)
-            nc.sync.dma_start(out=fr[:], in_=fr_v[gi])
+        def load_fr(gi, lo, hi):
+            if lo == 0:
+                tl[("fr", gi)] = work.tile([P, 4 * K], BF16, name="fr%d" % gi, tag="fr", bufs=IN_BUFS)
+            nc.sync.dma_start(out=tl[("fr", gi)][:, lo * K:hi * K], in_=fr_v[gi][:, lo * K:hi * K])
+
+        def load_mg(gi):
             mg = work.tile([P, 4 * F], BF16, name="mg%d" % gi, tag="mg", bufs=IN_BUFS)
             nc.sync.dma_start(out=mg[:], in_=m_v[gi])
-            tl[("fr", gi)] = fr
             tl[("mg", gi)] = mg
 
+        def load(gi):
+            load_fr(gi, 0, 4)
+            load_mg(gi)
+
+        load_fr(0, 0, 2)
+        load_mg(0)
+        load_fr(0, 2, 4)
         w_sb = const.tile([P, K], BF16, name="w_sb")
         nc.sync.dma_start(out=w_sb[:], in_=down_w)
-        load(0)
         load(1)
         load(2)
 
-        w_ps = psum.tile([P, 4, P], F32, name="w_ps", tag="a1", bufs=2)
+        w_ps = psum.tile([P, 4, P], F32, name="w_ps", tag="o", bufs=2)
         w_words = w_sb[:].bitcast(F32)
-        for c in range(4):
-            nc.tensor.transpose(out=w_ps[:, c, :], in_=w_words[:, c * P:(c + 1) * P], identity=ident[:])
         w_grp = const.tile([P, K], BF16, name="w_grp", align_bytes=64)
-        nc.vector.tensor_copy(
-            out=w_grp[:].bitcast(F32).rearrange("p (g n u) -> p g n u", g=2, u=2),
-            in_=w_ps[:].rearrange("p (g u) n -> p g n u", u=2),
-        )
         w_codes = const.tile([P, 2 * N], U32, name="w_codes", align_bytes=64)
         w_scales = const.tile([P, 2 * N], U8, name="w_scales", align_bytes=64)
-        nc.vector.quantize_mx(out=w_codes[:].bitcast(FP8X4), scales=w_scales[:], in_=w_grp[:])
+
+        def prep_w():
+            for c in range(4):
+                nc.tensor.transpose(out=w_ps[:, c, :], in_=w_words[:, c * P:(c + 1) * P], identity=ident[:])
+            nc.vector.tensor_copy(
+                out=w_grp[:].bitcast(F32).rearrange("p (g n u) -> p g n u", g=2, u=2),
+                in_=w_ps[:].rearrange("p (g u) n -> p g n u", u=2),
+            )
+            nc.vector.quantize_mx(out=w_codes[:].bitcast(FP8X4), scales=w_scales[:], in_=w_grp[:])
+
+        chunks = []
+        for gi in range(NG):
+            if gi == 0 or gi == NG - 1:
+                chunks.extend([(gi, h, 1) for h in range(4)])
+            else:
+                chunks.extend([(gi, 0, 2), (gi, 2, 2)])
+        NC = len(chunks)
 
         def ok(j):
-            return 0 <= j < NP
+            return 0 <= j < NC
 
-        def fr_bank(j, g, tag, bufs):
-            gi, h = divmod(j, 2)
-            words = tl[("fr", gi)][:].bitcast(F32)
-            bank = psum.tile([P, 512], F32, name="%s_%d_%d" % (tag, j, g), tag=tag, bufs=bufs)
+        def word_bank(j, src, row_words, first, tag, bufs, name):
+            gi, h0, nu = chunks[j]
+            words = tl[(src, gi)][:].bitcast(F32)
+            bank = psum.tile([P, 512], F32, name="%s%d" % (name, j), tag=tag, bufs=bufs)
             for u in range(2):
-                for unit in range(2):
-                    col = (2 * h + unit) * 512 + (2 * g + u) * P
-                    dst = (2 * u + unit) * P
+                for unit in range(nu):
+                    col = (h0 + unit) * row_words + first + u * P
+                    dst = (nu * u + unit) * P
                     nc.tensor.transpose(out=bank[:, dst:dst + P], in_=words[:, col:col + P], identity=ident[:])
             return bank
 
         def t1(j):
             for g in range(2):
-                tl[("a1", j, g)] = fr_bank(j, g, "a1", 2)
+                tl[("a1", j, g)] = word_bank(j, "fr", 512, 256 * g, "a1", 2, "a1_%d_" % g)
 
         def sq(j):
+            ne = 512 * chunks[j][2]
             t = work.tile([P, 2048], F32, name="sq%d" % j, tag="sq", bufs=3)
             for g in range(2):
-                nc.scalar.activation(out=t[:, g * 1024:(g + 1) * 1024], in_=tl[("a1", j, g)][:].bitcast(BF16), func=ACT.Square)
+                nc.scalar.activation(out=t[:, g * ne:(g + 1) * ne], in_=tl[("a1", j, g)][:, 0:ne // 2].bitcast(BF16), func=ACT.Square)
             tl[("sq", j)] = t
 
         def ad(j):
+            ne = 512 * chunks[j][2]
             t = tl[("sq", j)]
             q = work.tile([P, 1024], F32, name="q%d" % j, tag="q", bufs=4)
-            nc.gpsimd.tensor_tensor(out=q[:], in0=t[:, 0:1024], in1=t[:, 1024:2048], op=ALU.add)
-            nc.gpsimd.tensor_scalar(out=q[:], in0=q[:], scalar1=1.0, scalar2=EPS_MAG, op0=ALU.mult, op1=ALU.add)
+            nc.gpsimd.tensor_tensor(out=q[:, 0:ne], in0=t[:, 0:ne], in1=t[:, ne:2 * ne], op=ALU.add)
+            nc.gpsimd.tensor_scalar(out=q[:, 0:ne], in0=q[:, 0:ne], scalar1=1.0, scalar2=EPS_MAG, op0=ALU.mult, op1=ALU.add)
             tl[("q", j)] = q
 
         def r1(j):
+            ne = 512 * chunks[j][2]
             z = work.tile([P, 1024], F32, name="z%d" % j, tag="z", bufs=2)
-            nc.scalar.activation(out=z[:], in_=tl[("q", j)][:], func=ACT.Abs_reciprocal_sqrt, scale=KSC)
+            nc.scalar.activation(out=z[:, 0:ne], in_=tl[("q", j)][:, 0:ne], func=ACT.Abs_reciprocal_sqrt, scale=KSC)
             tl[("z", j)] = z
 
         def st(j):
+            ne = 512 * chunks[j][2]
             uu = work.tile([P, 1024], F32, name="uu%d" % j, tag="uu", bufs=3)
-            nc.vector.scalar_tensor_tensor(out=uu[:], in0=tl[("z", j)][:], scalar=1.0, in1=tl[("q", j)][:], op0=ALU.add, op1=ALU.mult)
+            nc.vector.scalar_tensor_tensor(out=uu[:, 0:ne], in0=tl[("z", j)][:, 0:ne], scalar=1.0, in1=tl[("q", j)][:, 0:ne], op0=ALU.add, op1=ALU.mult)
             tl[("uu", j)] = uu
 
         def r2(j):
+            ne = 512 * chunks[j][2]
             d = work.tile([P, 1024], F32, name="d%d" % j, tag="d", bufs=3)
-            nc.scalar.activation(out=d[:], in_=tl[("uu", j)][:], func=ACT.Abs_reciprocal_sqrt, bias=eps2[:])
+            nc.scalar.activation(
+                out=d[:, 0:ne].rearrange("p (w u e) -> p w u e", u=2, e=2),
+                in_=tl[("uu", j)][:, 0:ne].rearrange("p (u w e) -> p w u e", u=2, e=2),
+                func=ACT.Abs_reciprocal_sqrt,
+                bias=eps2[:],
+            )
             tl[("d", j)] = d
 
         def t3m(j):
-            gi, h = divmod(j, 2)
-            words = tl[("mg", gi)][:].bitcast(F32)
-            bank = psum.tile([P, 512], F32, name="mt%d" % j, tag="mt", bufs=1)
-            for u in range(2):
-                for unit in range(2):
-                    col = (2 * h + unit) * 256 + u * P
-                    dst = (2 * u + unit) * P
-                    nc.tensor.transpose(out=bank[:, dst:dst + P], in_=words[:, col:col + P], identity=ident[:])
-            tl[("mt", j)] = bank
+            tl[("mt", j)] = word_bank(j, "mg", 256, 0, "mt", 1, "mt")
 
         def t3a(j):
             for g in range(2):
-                tl[("a3", j, g)] = fr_bank(j, g, "a3", 3)
+                tl[("a3", j, g)] = word_bank(j, "fr", 512, 256 * g, "a3", 3, "a3_%d_" % g)
 
         def xm(j):
+            ne = 512 * chunks[j][2]
             s = work.tile([P, 1024], F32, name="s%d" % j, tag="s", bufs=2)
-            nc.vector.tensor_tensor(out=s[:], in0=tl[("mt", j)][:].bitcast(BF16), in1=tl[("d", j)][:], op=ALU.mult)
+            nc.vector.tensor_tensor(
+                out=s[:, 0:ne].rearrange("p (w u e) -> p w u e", u=2, e=2),
+                in0=tl[("mt", j)][:, 0:ne // 2].bitcast(BF16).rearrange("p (u w e) -> p w u e", u=2, e=2),
+                in1=tl[("d", j)][:, 0:ne].rearrange("p (w u e) -> p w u e", u=2, e=2),
+                op=ALU.mult,
+            )
             tl[("s", j)] = s
 
         def fn(j):
+            ne = 512 * chunks[j][2]
             grp = work.tile([P, 2048], BF16, name="grp%d" % j, tag="grp", bufs=3, align_bytes=64)
-            s4 = tl[("s", j)][:].rearrange("p (u w e) -> p w u e", u=2, e=2)
             for g in range(2):
                 nc.vector.tensor_tensor(
-                    out=grp[:, g * 1024:(g + 1) * 1024].rearrange("p (w u e) -> p w u e", u=2, e=2),
-                    in0=tl[("a3", j, g)][:].bitcast(BF16).rearrange("p (u w e) -> p w u e", u=2, e=2),
-                    in1=s4,
+                    out=grp[:, g * ne:(g + 1) * ne].rearrange("p (w u e) -> p w u e", u=2, e=2),
+                    in0=tl[("a3", j, g)][:, 0:ne // 2].bitcast(BF16).rearrange("p (u w e) -> p w u e", u=2, e=2),
+                    in1=tl[("s", j)][:, 0:ne].rearrange("p (w u e) -> p w u e", u=2, e=2),
                     op=ALU.mult,
                 )
             tl[("grp", j)] = grp
 
         def qz(j):
+            ne = 512 * chunks[j][2]
             codes = work.tile([P, 512], U32, name="codes%d" % j, tag="codes", bufs=3, align_bytes=64)
             scales = work.tile([P, 512], U8, name="scales%d" % j, tag="scales", bufs=3, align_bytes=64)
-            nc.vector.quantize_mx(out=codes[:].bitcast(FP8X4), scales=scales[:], in_=tl[("grp", j)][:])
+            nc.vector.quantize_mx(out=codes[:, 0:ne // 2].bitcast(FP8X4), scales=scales[:, 0:ne // 2], in_=tl[("grp", j)][:, 0:2 * ne])
             tl[("codes", j)] = codes
             tl[("scales", j)] = scales
 
         def mx(j):
-            gi, h = divmod(j, 2)
-            if h == 0:
-                tl[("o", gi)] = psum.tile([P, 512], F32, name="o%d" % gi, tag="o", bufs=2)
-            o = tl[("o", gi)]
+            nu = chunks[j][2]
+            o = psum.tile([P, 512], F32, name="o%d" % j, tag="o", bufs=2)
+            tl[("o", j)] = o
             codes = tl[("codes", j)]
             scales = tl[("scales", j)]
-            for unit in range(2):
-                col = (2 * h + unit) * P
+            for unit in range(nu):
                 for g in range(2):
-                    a = g * 256 + unit * P
+                    a = (g * nu + unit) * P
                     nc.tensor.matmul_mx(
-                        out=o[:, col:col + P],
+                        out=o[:, unit * N:(unit + 1) * N],
                         lhsT=codes[:, a:a + P].bitcast(FP8X4),
                         lhsT_scale=scales[:, a:a + P],
                         rhs=w_codes[:, g * N:(g + 1) * N].bitcast(FP8X4),
@@ -179,36 +204,41 @@ def tile_learnablespectralsinkhorn_pb_t_kernel(tc, freq_rect, processed_mag, dow
                         stop=(g == 1),
                     )
 
-        def oc(gi):
-            ob = work.tile([P, 512], F32, name="ob%d" % gi, tag="ob", bufs=2)
-            nc.scalar.copy(out=ob[:], in_=tl[("o", gi)][:])
-            nc.sync.dma_start(out=out_v[gi], in_=ob[:])
+        def oc(j):
+            gi, h0, nu = chunks[j]
+            ob = work.tile([P, 256], F32, name="ob%d" % j, tag="ob", bufs=3)
+            nc.scalar.copy(out=ob[:, 0:nu * N], in_=tl[("o", j)][:, 0:nu * N])
+            nc.sync.dma_start(out=out_v[gi][:, h0 * N:(h0 + nu) * N], in_=ob[:, 0:nu * N])
 
+        loaded = [2]
         t1(0)
-        for t in range(0, NP + 7):
+        for t in range(0, NC + 6):
             if ok(t):
                 sq(t)
             if ok(t + 1):
                 t1(t + 1)
             if ok(t):
                 ad(t)
-            if ok(t - 4):
-                xm(t - 4)
-            if ok(t - 3):
-                t3m(t - 3)
-            if ok(t - 5):
-                qz(t - 5)
-                mx(t - 5)
-            if ok(t - 4):
-                fn(t - 4)
-            if ok(t - 3):
-                t3a(t - 3)
             if ok(t - 2):
-                r1(t - 2)
                 st(t - 2)
+                r2(t - 2)
+            if t == 1:
+                prep_w()
             if ok(t - 3):
-                r2(t - 3)
-            if ok(t - 6) and (t - 6) % 2 == 1:
-                oc((t - 6) // 2)
-            if t % 2 == 0 and t // 2 + 3 < NG:
-                load(t // 2 + 3)
+                xm(t - 3)
+            if ok(t - 2):
+                t3m(t - 2)
+            if ok(t - 4):
+                qz(t - 4)
+                mx(t - 4)
+            if ok(t - 3):
+                fn(t - 3)
+            if ok(t - 2):
+                t3a(t - 2)
+            if ok(t - 5):
+                oc(t - 5)
+            if ok(t - 1):
+                r1(t - 1)
+            if ok(t) and chunks[t][0] + 3 > loaded[0] and loaded[0] + 1 < NG:
+                loaded[0] += 1
+                load(loaded[0])

@@ -24,6 +24,7 @@ EPS_DEN = 1e-6
 KSC = 1.0 / (4.0 * EPS_DEN * EPS_DEN)
 PINNED = True
 IN_BUFS = 6
+EPS_ON_ACT = 3
 
 
 def tile_learnablespectralsinkhorn_pb_t_kernel(tc, freq_rect, processed_mag, down_w, out):
@@ -41,6 +42,8 @@ def tile_learnablespectralsinkhorn_pb_t_kernel(tc, freq_rect, processed_mag, dow
 
         eps2 = const.tile([P, 1], F32, name="eps2")
         nc.vector.memset(eps2[:], EPS_DEN * EPS_DEN)
+        epsm = const.tile([P, 1], F32, name="epsm")
+        nc.vector.memset(epsm[:], EPS_MAG)
         warm = const.tile([P, 1], F32, name="warm")
         nc.scalar.activation(out=warm[:], in_=eps2[:], func=ACT.Abs_reciprocal_sqrt)
         ident = const.tile([P, P], F32, name="ident")
@@ -121,12 +124,15 @@ def tile_learnablespectralsinkhorn_pb_t_kernel(tc, freq_rect, processed_mag, dow
             t = tl[("sq", j)]
             q = work.tile([P, 1024], F32, name="q%d" % j, tag="q", bufs=4)
             nc.gpsimd.tensor_tensor(out=q[:, 0:ne], in0=t[:, 0:ne], in1=t[:, ne:2 * ne], op=ALU.add)
-            nc.gpsimd.tensor_scalar(out=q[:, 0:ne], in0=q[:, 0:ne], scalar1=1.0, scalar2=EPS_MAG, op0=ALU.mult, op1=ALU.add)
+            if j % EPS_ON_ACT != 1:
+                nc.gpsimd.tensor_scalar(out=q[:, 0:ne], in0=q[:, 0:ne], scalar1=1.0, scalar2=EPS_MAG, op0=ALU.mult, op1=ALU.add)
             tl[("q", j)] = q
 
         def r1(j):
             ne = 512 * chunks[j][2]
             z = work.tile([P, 1024], F32, name="z%d" % j, tag="z", bufs=2)
+            if j % EPS_ON_ACT == 1:
+                nc.scalar.activation(out=tl[("q", j)][:, 0:ne], in_=tl[("q", j)][:, 0:ne], func=ACT.Identity, bias=epsm[:])
             nc.scalar.activation(out=z[:, 0:ne], in_=tl[("q", j)][:, 0:ne], func=ACT.Abs_reciprocal_sqrt, scale=KSC)
             tl[("z", j)] = z
 

@@ -24,7 +24,6 @@ EPS_DEN = 1e-6
 KSC = 1.0 / (4.0 * EPS_DEN * EPS_DEN)
 PINNED = True
 IN_BUFS = 6
-EPS_ON_ACT = 3
 
 
 def tile_learnablespectralsinkhorn_pb_t_kernel(tc, freq_rect, processed_mag, down_w, out):
@@ -42,8 +41,6 @@ def tile_learnablespectralsinkhorn_pb_t_kernel(tc, freq_rect, processed_mag, dow
 
         eps2 = const.tile([P, 1], F32, name="eps2")
         nc.vector.memset(eps2[:], EPS_DEN * EPS_DEN)
-        epsm = const.tile([P, 1], F32, name="epsm")
-        nc.vector.memset(epsm[:], EPS_MAG)
         warm = const.tile([P, 1], F32, name="warm")
         nc.scalar.activation(out=warm[:], in_=eps2[:], func=ACT.Abs_reciprocal_sqrt)
         ident = const.tile([P, P], F32, name="ident")
@@ -124,15 +121,12 @@ def tile_learnablespectralsinkhorn_pb_t_kernel(tc, freq_rect, processed_mag, dow
             t = tl[("sq", j)]
             q = work.tile([P, 1024], F32, name="q%d" % j, tag="q", bufs=4)
             nc.gpsimd.tensor_tensor(out=q[:, 0:ne], in0=t[:, 0:ne], in1=t[:, ne:2 * ne], op=ALU.add)
-            if j % EPS_ON_ACT != 1:
-                nc.gpsimd.tensor_scalar(out=q[:, 0:ne], in0=q[:, 0:ne], scalar1=1.0, scalar2=EPS_MAG, op0=ALU.mult, op1=ALU.add)
+            nc.gpsimd.tensor_scalar(out=q[:, 0:ne], in0=q[:, 0:ne], scalar1=1.0, scalar2=EPS_MAG, op0=ALU.mult, op1=ALU.add)
             tl[("q", j)] = q
 
         def r1(j):
             ne = 512 * chunks[j][2]
             z = work.tile([P, 1024], F32, name="z%d" % j, tag="z", bufs=2)
-            if j % EPS_ON_ACT == 1:
-                nc.scalar.activation(out=tl[("q", j)][:, 0:ne], in_=tl[("q", j)][:, 0:ne], func=ACT.Identity, bias=epsm[:])
             nc.scalar.activation(out=z[:, 0:ne], in_=tl[("q", j)][:, 0:ne], func=ACT.Abs_reciprocal_sqrt, scale=KSC)
             tl[("z", j)] = z
 
@@ -213,7 +207,7 @@ def tile_learnablespectralsinkhorn_pb_t_kernel(tc, freq_rect, processed_mag, dow
         def oc(j):
             gi, h0, nu = chunks[j]
             ob = work.tile([P, 256], F32, name="ob%d" % j, tag="ob", bufs=3)
-            nc.scalar.copy(out=ob[:, 0:nu * N], in_=tl[("o", j)][:, 0:nu * N])
+            nc.vector.tensor_copy(out=ob[:, 0:nu * N], in_=tl[("o", j)][:, 0:nu * N])
             nc.sync.dma_start(out=out_v[gi][:, h0 * N:(h0 + nu) * N], in_=ob[:, 0:nu * N])
 
         loaded = [2]

@@ -22,7 +22,7 @@ NP = 2 * NG
 EPS_MAG = 1e-8
 EPS_DEN = 1e-6
 KSC = 1.0 / (4.0 * EPS_DEN * EPS_DEN)
-PINNED = True
+PINNED = False
 IN_BUFS = 6
 
 
@@ -207,7 +207,7 @@ def tile_learnablespectralsinkhorn_pb_t_kernel(tc, freq_rect, processed_mag, dow
         def oc(j):
             gi, h0, nu = chunks[j]
             ob = work.tile([P, 256], F32, name="ob%d" % j, tag="ob", bufs=3)
-            nc.vector.tensor_copy(out=ob[:, 0:nu * N], in_=tl[("o", j)][:, 0:nu * N])
+            nc.scalar.copy(out=ob[:, 0:nu * N], in_=tl[("o", j)][:, 0:nu * N])
             nc.sync.dma_start(out=out_v[gi][:, h0 * N:(h0 + nu) * N], in_=ob[:, 0:nu * N])
 
         loaded = [2]

@@ -22,7 +22,7 @@ NP = 2 * NG
 EPS_MAG = 1e-8
 EPS_DEN = 1e-6
 KSC = 1.0 / (4.0 * EPS_DEN * EPS_DEN)
-PINNED = False
+PINNED = True
 IN_BUFS = 6
 
 
@@ -41,6 +41,8 @@ def tile_learnablespectralsinkhorn_pb_t_kernel(tc, freq_rect, processed_mag, dow
 
         eps2 = const.tile([P, 1], F32, name="eps2")
         nc.vector.memset(eps2[:], EPS_DEN * EPS_DEN)
+        keps = const.tile([P, 1], F32, name="keps")
+        nc.vector.memset(keps[:], KSC * EPS_MAG)
         warm = const.tile([P, 1], F32, name="warm")
         nc.scalar.activation(out=warm[:], in_=eps2[:], func=ACT.Abs_reciprocal_sqrt)
         ident = const.tile([P, P], F32, name="ident")
@@ -121,19 +123,23 @@ def tile_learnablespectralsinkhorn_pb_t_kernel(tc, freq_rect, processed_mag, dow
             t = tl[("sq", j)]
             q = work.tile([P, 1024], F32, name="q%d" % j, tag="q", bufs=4)
             nc.gpsimd.tensor_tensor(out=q[:, 0:ne], in0=t[:, 0:ne], in1=t[:, ne:2 * ne], op=ALU.add)
-            nc.gpsimd.tensor_scalar(out=q[:, 0:ne], in0=q[:, 0:ne], scalar1=1.0, scalar2=EPS_MAG, op0=ALU.mult, op1=ALU.add)
             tl[("q", j)] = q
 
         def r1(j):
             ne = 512 * chunks[j][2]
-            z = work.tile([P, 1024], F32, name="z%d" % j, tag="z", bufs=2)
-            nc.scalar.activation(out=z[:, 0:ne], in_=tl[("q", j)][:, 0:ne], func=ACT.Abs_reciprocal_sqrt, scale=KSC)
+            z = work.tile([P, 1024], F32, name="z%d" % j, tag="z", bufs=3)
+            nc.scalar.activation(out=z[:, 0:ne], in_=tl[("q", j)][:, 0:ne], func=ACT.Abs_reciprocal_sqrt, scale=KSC, bias=keps[:])
             tl[("z", j)] = z
+
+        def z1(j):
+            ne = 512 * chunks[j][2]
+            z = tl[("z", j)]
+            nc.gpsimd.tensor_scalar(out=z[:, 0:ne], in0=z[:, 0:ne], scalar1=1.0, scalar2=1.0, op0=ALU.mult, op1=ALU.add)
 
         def st(j):
             ne = 512 * chunks[j][2]
             uu = work.tile([P, 1024], F32, name="uu%d" % j, tag="uu", bufs=3)
-            nc.vector.scalar_tensor_tensor(out=uu[:, 0:ne], in0=tl[("z", j)][:, 0:ne], scalar=1.0, in1=tl[("q", j)][:, 0:ne], op0=ALU.add, op1=ALU.mult)
+            nc.vector.scalar_tensor_tensor(out=uu[:, 0:ne], in0=tl[("q", j)][:, 0:ne], scalar=EPS_MAG, in1=tl[("z", j)][:, 0:ne], op0=ALU.add, op1=ALU.mult)
             tl[("uu", j)] = uu
 
         def r2(j):
@@ -212,31 +218,34 @@ def tile_learnablespectralsinkhorn_pb_t_kernel(tc, freq_rect, processed_mag, dow
 
         loaded = [2]
         t1(0)
-        for t in range(0, NC + 6):
+        for t in range(0, NC + 7):
             if ok(t):
                 sq(t)
             if ok(t + 1):
                 t1(t + 1)
+            if ok(t - 2):
+                z1(t - 2)
             if ok(t):
                 ad(t)
-            if ok(t - 2):
-                st(t - 2)
-                r2(t - 2)
             if t == 1:
                 prep_w()
-            if ok(t - 3):
-                xm(t - 3)
-            if ok(t - 2):
-                t3m(t - 2)
             if ok(t - 4):
-                qz(t - 4)
-                mx(t - 4)
+                xm(t - 4)
             if ok(t - 3):
-                fn(t - 3)
+                t3m(t - 3)
             if ok(t - 2):
-                t3a(t - 2)
+                st(t - 2)
+            if ok(t - 3):
+                r2(t - 3)
             if ok(t - 5):
-                oc(t - 5)
+                qz(t - 5)
+                mx(t - 5)
+            if ok(t - 4):
+                fn(t - 4)
+            if ok(t - 3):
+                t3a(t - 3)
+            if ok(t - 6):
+                oc(t - 6)
             if ok(t - 1):
                 r1(t - 1)
             if ok(t) and chunks[t][0] + 3 > loaded[0] and loaded[0] + 1 < NG:

from contextlib import ExitStack

import concourse.mybir as mybir
from concourse.masks import make_identity

F32 = mybir.dt.float32
BF16 = mybir.dt.bfloat16
U32 = mybir.dt.uint32
U8 = mybir.dt.uint8
FP8X4 = mybir.dt.float8_e4m3fn_x4
ACT = mybir.ActivationFunctionType
ALU = mybir.AluOpType

P = 128
ROWS = 8192
K = 1024
F = 512
N = 128
FLOPS = 2 * ROWS * K * N
NG = ROWS // (4 * P)
NP = 2 * NG
EPS_MAG = 1e-8
EPS_DEN = 1e-6
KSC = 1.0 / (4.0 * EPS_DEN * EPS_DEN)
PINNED = True
IN_BUFS = 6


def tile_learnablespectralsinkhorn_pb_t_kernel(tc, freq_rect, processed_mag, down_w, out):
    nc = tc.nc
    fr_v = freq_rect.flatten_outer_dims().rearrange("(g p j) k -> g p (j k)", p=P, j=4)
    m_v = processed_mag.flatten_outer_dims().rearrange("(g p j) f -> g p (j f)", p=P, j=4)
    out_v = out.flatten_outer_dims().rearrange("(g p j) n -> g p (j n)", p=P, j=4)
    tl = {}
    with ExitStack() as ctx:
        const = ctx.enter_context(tc.tile_pool(name="const", bufs=1))
        work = ctx.enter_context(tc.tile_pool(name="work", bufs=2))
        psum = ctx.enter_context(tc.psum_pool(name="psum", bufs=2))
        if PINNED:
            ctx.enter_context(tc.manual_schedule())

        eps2 = const.tile([P, 1], F32, name="eps2")
        nc.vector.memset(eps2[:], EPS_DEN * EPS_DEN)
        keps = const.tile([P, 1], F32, name="keps")
        nc.vector.memset(keps[:], KSC * EPS_MAG)
        warm = const.tile([P, 1], F32, name="warm")
        nc.scalar.activation(out=warm[:], in_=eps2[:], func=ACT.Abs_reciprocal_sqrt)
        ident = const.tile([P, P], F32, name="ident")
        make_identity(nc, ident[:])

        def load_fr(gi, lo, hi):
            if lo == 0:
                tl[("fr", gi)] = work.tile([P, 4 * K], BF16, name="fr%d" % gi, tag="fr", bufs=IN_BUFS)
            nc.sync.dma_start(out=tl[("fr", gi)][:, lo * K:hi * K], in_=fr_v[gi][:, lo * K:hi * K])

        def load_mg(gi):
            mg = work.tile([P, 4 * F], BF16, name="mg%d" % gi, tag="mg", bufs=IN_BUFS)
            nc.sync.dma_start(out=mg[:], in_=m_v[gi])
            tl[("mg", gi)] = mg

        def load(gi):
            load_fr(gi, 0, 4)
            load_mg(gi)

        load_fr(0, 0, 2)
        load_mg(0)
        load_fr(0, 2, 4)
        w_sb = const.tile([P, K], BF16, name="w_sb")
        nc.sync.dma_start(out=w_sb[:], in_=down_w)
        load(1)
        load(2)

        w_ps = psum.tile([P, 4, P], F32, name="w_ps", tag="o", bufs=2)
        w_words = w_sb[:].bitcast(F32)
        w_grp = const.tile([P, K], BF16, name="w_grp", align_bytes=64)
        w_codes = const.tile([P, 2 * N], U32, name="w_codes", align_bytes=64)
        w_scales = const.tile([P, 2 * N], U8, name="w_scales", align_bytes=64)

        def prep_w():
            for c in range(4):
                nc.tensor.transpose(out=w_ps[:, c, :], in_=w_words[:, c * P:(c + 1) * P], identity=ident[:])
            nc.vector.tensor_copy(
                out=w_grp[:].bitcast(F32).rearrange("p (g n u) -> p g n u", g=2, u=2),
                in_=w_ps[:].rearrange("p (g u) n -> p g n u", u=2),
            )
            nc.vector.quantize_mx(out=w_codes[:].bitcast(FP8X4), scales=w_scales[:], in_=w_grp[:])

        chunks = []
        for gi in range(NG):
            if gi == 0 or gi == NG - 1:
                chunks.extend([(gi, h, 1) for h in range(4)])
            else:
                chunks.extend([(gi, 0, 2), (gi, 2, 2)])
        NC = len(chunks)

        def ok(j):
            return 0 <= j < NC

        def word_bank(j, src, row_words, first, tag, bufs, name):
            gi, h0, nu = chunks[j]
            words = tl[(src, gi)][:].bitcast(F32)
            bank = psum.tile([P, 512], F32, name="%s%d" % (name, j), tag=tag, bufs=bufs)
            for u in range(2):
                for unit in range(nu):
                    col = (h0 + unit) * row_words + first + u * P
                    dst = (nu * u + unit) * P
                    nc.tensor.transpose(out=bank[:, dst:dst + P], in_=words[:, col:col + P], identity=ident[:])
            return bank

        def t1(j):
            for g in range(2):
                tl[("a1", j, g)] = word_bank(j, "fr", 512, 256 * g, "a1", 2, "a1_%d_" % g)

        def sq(j):
            ne = 512 * chunks[j][2]
            t = work.tile([P, 2048], F32, name="sq%d" % j, tag="sq", bufs=3)
            for g in range(2):
                nc.scalar.activation(out=t[:, g * ne:(g + 1) * ne], in_=tl[("a1", j, g)][:, 0:ne // 2].bitcast(BF16), func=ACT.Square)
            tl[("sq", j)] = t

        def ad(j):
            ne = 512 * chunks[j][2]
            t = tl[("sq", j)]
            q = work.tile([P, 1024], F32, name="q%d" % j, tag="q", bufs=4)
            nc.gpsimd.tensor_tensor(out=q[:, 0:ne], in0=t[:, 0:ne], in1=t[:, ne:2 * ne], op=ALU.add)
            tl[("q", j)] = q

        def r1(j):
            ne = 512 * chunks[j][2]
            z = work.tile([P, 1024], F32, name="z%d" % j, tag="z", bufs=3)
            nc.scalar.activation(out=z[:, 0:ne], in_=tl[("q", j)][:, 0:ne], func=ACT.Abs_reciprocal_sqrt, scale=KSC, bias=keps[:])
            tl[("z", j)] = z

        def z1(j):
            ne = 512 * chunks[j][2]
            z = tl[("z", j)]
            nc.gpsimd.tensor_scalar(out=z[:, 0:ne], in0=z[:, 0:ne], scalar1=1.0, scalar2=1.0, op0=ALU.mult, op1=ALU.add)

        def st(j):
            ne = 512 * chunks[j][2]
            uu = work.tile([P, 1024], F32, name="uu%d" % j, tag="uu", bufs=3)
            nc.vector.scalar_tensor_tensor(out=uu[:, 0:ne], in0=tl[("q", j)][:, 0:ne], scalar=EPS_MAG, in1=tl[("z", j)][:, 0:ne], op0=ALU.add, op1=ALU.mult)
            tl[("uu", j)] = uu

        def r2(j):
            ne = 512 * chunks[j][2]
            d = work.tile([P, 1024], F32, name="d%d" % j, tag="d", bufs=3)
            nc.scalar.activation(
                out=d[:, 0:ne].rearrange("p (w u e) -> p w u e", u=2, e=2),
                in_=tl[("uu", j)][:, 0:ne].rearrange("p (u w e) -> p w u e", u=2, e=2),
                func=ACT.Abs_reciprocal_sqrt,
                bias=eps2[:],
            )
            tl[("d", j)] = d

        def t3m(j):
            tl[("mt", j)] = word_bank(j, "mg", 256, 0, "mt", 1, "mt")

        def t3a(j):
            for g in range(2):
                tl[("a3", j, g)] = word_bank(j, "fr", 512, 256 * g, "a3", 3, "a3_%d_" % g)

        def xm(j):
            ne = 512 * chunks[j][2]
            s = work.tile([P, 1024], F32, name="s%d" % j, tag="s", bufs=2)
            nc.vector.tensor_tensor(
                out=s[:, 0:ne].rearrange("p (w u e) -> p w u e", u=2, e=2),
                in0=tl[("mt", j)][:, 0:ne // 2].bitcast(BF16).rearrange("p (u w e) -> p w u e", u=2, e=2),
                in1=tl[("d", j)][:, 0:ne].rearrange("p (w u e) -> p w u e", u=2, e=2),
                op=ALU.mult,
            )
            tl[("s", j)] = s

        def fn(j):
            ne = 512 * chunks[j][2]
            grp = work.tile([P, 2048], BF16, name="grp%d" % j, tag="grp", bufs=3, align_bytes=64)
            for g in range(2):
                nc.vector.tensor_tensor(
                    out=grp[:, g * ne:(g + 1) * ne].rearrange("p (w u e) -> p w u e", u=2, e=2),
                    in0=tl[("a3", j, g)][:, 0:ne // 2].bitcast(BF16).rearrange("p (u w e) -> p w u e", u=2, e=2),
                    in1=tl[("s", j)][:, 0:ne].rearrange("p (w u e) -> p w u e", u=2, e=2),
                    op=ALU.mult,
                )
            tl[("grp", j)] = grp

        def qz(j):
            ne = 512 * chunks[j][2]
            codes = work.tile([P, 512], U32, name="codes%d" % j, tag="codes", bufs=3, align_bytes=64)
            scales = work.tile([P, 512], U8, name="scales%d" % j, tag="scales", bufs=3, align_bytes=64)
            nc.vector.quantize_mx(out=codes[:, 0:ne // 2].bitcast(FP8X4), scales=scales[:, 0:ne // 2], in_=tl[("grp", j)][:, 0:2 * ne])
            tl[("codes", j)] = codes
            tl[("scales", j)] = scales

        def mx(j):
            nu = chunks[j][2]
            o = psum.tile([P, 512], F32, name="o%d" % j, tag="o", bufs=2)
            tl[("o", j)] = o
            codes = tl[("codes", j)]
            scales = tl[("scales", j)]
            for unit in range(nu):
                for g in range(2):
                    a = (g * nu + unit) * P
                    nc.tensor.matmul_mx(
                        out=o[:, unit * N:(unit + 1) * N],
                        lhsT=codes[:, a:a + P].bitcast(FP8X4),
                        lhsT_scale=scales[:, a:a + P],
                        rhs=w_codes[:, g * N:(g + 1) * N].bitcast(FP8X4),
                        rhs_scale=w_scales[:, g * N:(g + 1) * N],
                        start=(g == 0),
                        stop=(g == 1),
                    )

        def oc(j):
            gi, h0, nu = chunks[j]
            ob = work.tile([P, 256], F32, name="ob%d" % j, tag="ob", bufs=3)
            nc.scalar.copy(out=ob[:, 0:nu * N], in_=tl[("o", j)][:, 0:nu * N])
            nc.sync.dma_start(out=out_v[gi][:, h0 * N:(h0 + nu) * N], in_=ob[:, 0:nu * N])

        loaded = [2]
        t1(0)
        for t in range(0, NC + 7):
            if ok(t):
                sq(t)
            if ok(t + 1):
                t1(t + 1)
            if ok(t - 2):
                z1(t - 2)
            if ok(t):
                ad(t)
            if t == 1:
                prep_w()
            if ok(t - 4):
                xm(t - 4)
            if ok(t - 3):
                t3m(t - 3)
            if ok(t - 2):
                st(t - 2)
            if ok(t - 3):
                r2(t - 3)
            if ok(t - 5):
                qz(t - 5)
                mx(t - 5)
            if ok(t - 4):
                fn(t - 4)
            if ok(t - 3):
                t3a(t - 3)
            if ok(t - 6):
                oc(t - 6)
            if ok(t - 1):
                r1(t - 1)
            if ok(t) and chunks[t][0] + 3 > loaded[0] and loaded[0] + 1 < NG:
                loaded[0] += 1
                load(loaded[0])
